import numpy as np
import ml_dtypes


def mxq(x, axis, fmt="e4m3"):
    dtype, down = {"e4m3": (ml_dtypes.float8_e4m3fn, 7), "e5m2": (ml_dtypes.float8_e5m2, 14)}[fmt]
    v = np.moveaxis(np.asarray(x, np.float32).astype(ml_dtypes.bfloat16).astype(np.float64), axis, -1)
    blocks = v.reshape(v.shape[:-1] + (-1, 32))
    amax = np.abs(blocks).max(-1, keepdims=True)
    byte = np.maximum(np.where(amax > 0, np.frexp(amax)[1] - 1 + 127, 0) - down, 1)
    scale = np.exp2(byte - 127.0)
    codes = (blocks / scale).astype(np.float32).astype(dtype).astype(np.float64)
    return np.moveaxis((codes * scale).reshape(v.shape), -1, axis)


WIDE = False


def mx_kscale(k):
    if not WIDE:
        return np.ones(k)
    levels = np.array([20, -20, 10, -10, 0])
    a = np.random.permutation(np.resize(levels, k // 512 * 4)).reshape(k // 512, 4)
    idx = np.arange(k)
    return np.exp2(a[idx // 512, idx % 128 // 32])


BF16 = ml_dtypes.bfloat16


def bf(x):
    return np.asarray(x, np.float32).astype(BF16)


def f64(x):
    return np.asarray(x).astype(np.float64)


B, H, T, S, D = 2, 4, 1024, 512, 512


def setup_inputs():
    s = mx_kscale(T)
    aw = np.random.uniform(0.0, 1.0, (B, H, T, S))
    aw = aw / aw.sum(-1, keepdims=True)
    v = np.random.standard_normal((B, H, S, D)) * 8.0
    g = np.random.standard_normal((B, T, H * D)) * np.exp2(np.random.randint(-12, 1, (B, T, 1))) * 128.0
    return {"attn_weights": bf(aw * s[:, None]), "v": bf(v), "batch_size": B, "tgt_len": T,
            "grad_out": bf(g / s[None, :, None])}


def reference(attn_weights, v, batch_size, tgt_len, grad_out):
    aw = f64(attn_weights)
    heads = aw.shape[1]
    head_dim = np.asarray(v).shape[-1]
    g = f64(grad_out).reshape(batch_size, tgt_len, heads, head_dim).transpose(0, 2, 1, 3)
    awq = mxq(aw, 2, "e4m3")
    gq = mxq(g, 2, "e5m2")
    return awq.transpose(0, 1, 3, 2) @ gq

@@ -1,0 +1,198 @@
+from contextlib import ExitStack
+
+import concourse.mybir as mybir
+
+BF16 = mybir.dt.bfloat16
+F32 = mybir.dt.float32
+U32 = mybir.dt.uint32
+U8 = mybir.dt.uint8
+E4M3X4 = mybir.dt.float8_e4m3fn_x4
+E5M2X4 = mybir.dt.float8_e5m2_x4
+
+P = 128
+PACK = 4
+B, H, T, S, D = 2, 4, 1024, 512, 512
+PASSES = T // (P * PACK)
+M_TILES = S // P
+HEADS = B * H
+
+FLOPS = 2 * B * H * S * D * T
+BYTES = 2 * B * H * T * S + 2 * B * T * H * D + 4 * B * H * S * D
+
+S_COLS = 112
+S_COLS_BY_HEAD = {4: 0}
+
+
+def tile_attentionweightedvalues_kernel(tc, attn_weights, v, batch_size, tgt_len, grad_out, out):
+    nc = tc.nc
+    with ExitStack() as ctx:
+        a_raw_pool = ctx.enter_context(tc.tile_pool(name="a_raw", bufs=4))
+        g_raw_pool = ctx.enter_context(tc.tile_pool(name="g_raw", bufs=3))
+        grp_v_pool = ctx.enter_context(tc.tile_pool(name="grp_v", bufs=6))
+        grp_s_pool = ctx.enter_context(tc.tile_pool(name="grp_s", bufs=4))
+        a_mx_pool = ctx.enter_context(tc.tile_pool(name="a_mx", bufs=3))
+        g_mx_pool = ctx.enter_context(tc.tile_pool(name="g_mx", bufs=1))
+        stage_pool = ctx.enter_context(tc.tile_pool(name="stage", bufs=6))
+        psum_pool = ctx.enter_context(tc.psum_pool(name="acc", bufs=8))
+        ctx.enter_context(tc.manual_schedule())
+
+        a_raw = {}
+        g_raw = {}
+        grouped = {}
+        a_mx = {}
+        g_mx = {}
+        acc = {}
+        stage = {}
+
+        def load_a(k, split):
+            raw = a_raw_pool.tile([P, PASSES, PACK, S], BF16, name="a_raw")
+            a_raw[k] = raw
+            src = attn_weights[k // H, k % H].rearrange("(c p j) w -> p c j w", c=PASSES, p=P, j=PACK)
+            if split:
+                for c in range(PASSES):
+                    nc.sync.dma_start(out=raw[:, c], in_=src[:, c])
+            else:
+                nc.sync.dma_start(out=raw[:], in_=src)
+
+        def load_g(b, c):
+            raw = g_raw_pool.tile([P, PACK, H, D], BF16, name="g_raw")
+            g_raw[(b, c)] = raw
+            rows = grad_out[b, c * P * PACK : (c + 1) * P * PACK, :]
+            nc.sync.dma_start(out=raw[:], in_=rows.rearrange("(p j) (h d) -> p j h d", j=PACK, h=H))
+
+        def regroup(copy, dst, src, lo, hi):
+            copy(
+                out=dst[:, PACK * lo : PACK * hi].rearrange("p (c i t) -> p c t i", i=4, t=PACK),
+                in_=src[:, :, lo:hi].rearrange("p t (c i) -> p c t i", i=4),
+            )
+
+        def s_cols(k):
+            return S_COLS_BY_HEAD.get(k, S_COLS)
+
+        def a_regroup_scalar(k):
+            for c in range(PASSES):
+                grouped[("a", k, c)] = grp_v_pool.tile([P, PACK * S], BF16, name="grp_v", align_bytes=64)
+                if s_cols(k) > 0:
+                    regroup(nc.scalar.copy, grouped[("a", k, c)], a_raw[k][:, c], S - s_cols(k), S)
+
+        def a_regroup_vector(k):
+            for c in range(PASSES):
+                regroup(nc.vector.tensor_copy, grouped[("a", k, c)], a_raw[k][:, c], 0, S - s_cols(k))
+
+        def a_quantise(k):
+            codes = a_mx_pool.tile([P, PASSES, S], U32, name="a_codes", align_bytes=64)
+            scales = a_mx_pool.tile([P, PASSES, S], U8, name="a_scales", align_bytes=64)
+            a_mx[k] = (codes, scales)
+            for c in range(PASSES):
+                nc.vector.quantize_mx(
+                    out=codes[:, c, :].bitcast(E4M3X4), scales=scales[:, c, :], in_=grouped[("a", k, c)][:]
+                )
+
+        def g_regroup(b, c, h, on_vector):
+            if on_vector:
+                dst = grp_v_pool.tile([P, PACK * D], BF16, name="grp_v", align_bytes=64)
+                regroup(nc.vector.tensor_copy, dst, g_raw[(b, c)][:, :, h, :], 0, D)
+            else:
+                dst = grp_s_pool.tile([P, PACK * D], BF16, name="grp_s", align_bytes=64)
+                regroup(nc.scalar.copy, dst, g_raw[(b, c)][:, :, h, :], 0, D)
+            grouped[("g", b, c, h)] = dst
+
+        def g_quantise(b, c, h):
+            codes = g_mx_pool.tile([P, D], U32, name="g_codes_%d_%d_%d" % (b, c, h), align_bytes=64)
+            scales = g_mx_pool.tile([P, D], U8, name="g_scales_%d_%d_%d" % (b, c, h), align_bytes=64)
+            g_mx[(b, c, h)] = (codes, scales)
+            nc.vector.quantize_mx(out=codes[:].bitcast(E5M2X4), scales=scales[:], in_=grouped[("g", b, c, h)][:])
+
+        def mx_pass(k, m, c):
+            if c == 0:
+                acc[(k, m)] = psum_pool.tile([P, D], F32, name="acc")
+            a_codes, a_scales = a_mx[k]
+            g_codes, g_scales = g_mx[(k // H, c, k % H)]
+            cols = slice(m * P, (m + 1) * P)
+            nc.tensor.matmul_mx(
+                out=acc[(k, m)][:],
+                lhsT=a_codes[:, c, cols].bitcast(E4M3X4),
+                lhsT_scale=a_scales[:, c, cols],
+                rhs=g_codes[:].bitcast(E5M2X4),
+                rhs_scale=g_scales[:],
+                start=(c == 0),
+                stop=(c == PASSES - 1),
+            )
+
+        def multiply(k):
+            for m in range(M_TILES):
+                for c in range(PASSES):
+                    mx_pass(k, m, c)
+
+        def evict(k, m, copy):
+            if m == 0:
+                stage[k] = stage_pool.tile([P, M_TILES, D], F32, name="stage")
+            copy(out=stage[k][:, m, :], in_=acc[(k, m)][:])
+
+        def evict_head(k):
+            for m in range(M_TILES):
+                evict(k, m, nc.scalar.copy)
+
+        def store(k, m_lo, m_hi):
+            dst = out[k // H, k % H].rearrange("(m p) d -> p m d", p=P)
+            nc.sync.dma_start(out=dst[:, m_lo:m_hi, :], in_=stage[k][:, m_lo:m_hi, :])
+
+        load_a(0, True)
+        load_g(0, 0)
+        load_g(0, 1)
+        load_a(1, False)
+        load_a(2, False)
+        load_a(3, False)
+        load_g(1, 0)
+        a_regroup_scalar(0)
+        a_regroup_vector(0)
+        a_quantise(0)
+        load_a(4, False)
+        for b in range(B):
+            first = b * H
+            for c in range(PASSES):
+                g_regroup(b, c, 2, False)
+                if b == 1 and c == 0:
+                    evict_head(first - 1)
+                g_regroup(b, c, 3, False)
+                g_regroup(b, c, 0, True)
+                g_regroup(b, c, 1, True)
+                g_quantise(b, c, 0)
+                g_quantise(b, c, 1)
+                if b == 0 and c == 0:
+                    load_g(1, 1)
+            if b == 0:
+                a_regroup_scalar(1)
+            else:
+                for k in range(H):
+                    store(k, 0, M_TILES)
+                a_regroup_scalar(first)
+                a_regroup_vector(first)
+                a_quantise(first)
+                a_regroup_scalar(first + 1)
+            multiply(first)
+            for k in range(first + 1, first + H):
+                h = k % H
+                a_regroup_vector(k)
+                if h >= 2:
+                    g_quantise(b, 0, h)
+                    g_quantise(b, 1, h)
+                a_quantise(k)
+                if b == 0:
+                    load_a(k + H, False)
+                evict_head(k - 1)
+                if b == 1:
+                    store(k - 1, 0, M_TILES)
+                if k < first + H - 1:
+                    a_regroup_scalar(k + 1)
+                if k < HEADS - 1:
+                    multiply(k)
+                else:
+                    for c in range(PASSES):
+                        for m in range(M_TILES):
+                            mx_pass(k, m, c)
+        last = HEADS - 1
+        for m in range(M_TILES):
+            evict(last, m, nc.vector.tensor_copy if m % 2 == 0 else nc.scalar.copy)
+            if m % 2 == 1:
+                store(last, m - 1, m + 1)

@@ -19,8 +19,8 @@ HEADS = B * H
 FLOPS = 2 * B * H * S * D * T
 BYTES = 2 * B * H * T * S + 2 * B * T * H * D + 4 * B * H * S * D
 
-S_COLS = 112
-S_COLS_BY_HEAD = {4: 0}
+S_ROWS = 28
+S_ROWS_BY_HEAD = {0: 44, 1: 44, 4: 0}
 
 
 def tile_attentionweightedvalues_kernel(tc, attn_weights, v, batch_size, tgt_len, grad_out, out):
@@ -66,27 +66,50 @@ def tile_attentionweightedvalues_kernel(tc, attn_weights, v, batch_size, tgt_len
                 in_=src[:, :, lo:hi].rearrange("p t (c i) -> p c t i", i=4),
             )
 
-        def s_cols(k):
-            return S_COLS_BY_HEAD.get(k, S_COLS)
+        def v_rows(k):
+            return P - S_ROWS_BY_HEAD.get(k, S_ROWS)
 
         def a_regroup_scalar(k):
             for c in range(PASSES):
-                grouped[("a", k, c)] = grp_v_pool.tile([P, PACK * S], BF16, name="grp_v", align_bytes=64)
-                if s_cols(k) > 0:
-                    regroup(nc.scalar.copy, grouped[("a", k, c)], a_raw[k][:, c], S - s_cols(k), S)
+                dst = grp_v_pool.tile([P, PACK * S], BF16, name="grp_v", align_bytes=64)
+                grouped[("a", k, c)] = dst
+                if v_rows(k) < P:
+                    nc.scalar.copy(
+                        out=dst[:]
+                        .rearrange("p (m i j) -> p m i j", m=M_TILES, i=P, j=PACK)[:, :, v_rows(k) : P, :]
+                        .rearrange("p m i j -> p i j m"),
+                        in_=a_raw[k][:, c]
+                        .rearrange("p j (i m) -> p j i m", m=M_TILES)[:, :, v_rows(k) : P, :]
+                        .rearrange("p j i m -> p i j m"),
+                    )
+
+        def a_regroup_vector_pass(k, c):
+            nc.vector.tensor_copy(
+                out=grouped[("a", k, c)][:]
+                .rearrange("p (mh ml i j) -> p mh ml i j", mh=2, ml=2, i=P, j=PACK)[:, :, :, 0 : v_rows(k), :]
+                .rearrange("p mh ml i j -> p mh i j ml"),
+                in_=a_raw[k][:, c]
+                .rearrange("p j (i mh ml) -> p j i mh ml", mh=2, ml=2)[:, :, 0 : v_rows(k), :, :]
+                .rearrange("p j i mh ml -> p mh i j ml"),
+            )
 
         def a_regroup_vector(k):
             for c in range(PASSES):
-                regroup(nc.vector.tensor_copy, grouped[("a", k, c)], a_raw[k][:, c], 0, S - s_cols(k))
+                a_regroup_vector_pass(k, c)
+
+        def a_quantise_pass(k, c):
+            if c == 0:
+                codes = a_mx_pool.tile([P, PASSES, S], U32, name="a_codes", align_bytes=64)
+                scales = a_mx_pool.tile([P, PASSES, S], U8, name="a_scales", align_bytes=64)
+                a_mx[k] = (codes, scales)
+            codes, scales = a_mx[k]
+            nc.vector.quantize_mx(
+                out=codes[:, c, :].bitcast(E4M3X4), scales=scales[:, c, :], in_=grouped[("a", k, c)][:]
+            )
 
         def a_quantise(k):
-            codes = a_mx_pool.tile([P, PASSES, S], U32, name="a_codes", align_bytes=64)
-            scales = a_mx_pool.tile([P, PASSES, S], U8, name="a_scales", align_bytes=64)
-            a_mx[k] = (codes, scales)
             for c in range(PASSES):
-                nc.vector.quantize_mx(
-                    out=codes[:, c, :].bitcast(E4M3X4), scales=scales[:, c, :], in_=grouped[("a", k, c)][:]
-                )
+                a_quantise_pass(k, c)
 
         def g_regroup(b, c, h, on_vector):
             if on_vector:
@@ -134,64 +157,77 @@ def tile_attentionweightedvalues_kernel(tc, attn_weights, v, batch_size, tgt_len
                 evict(k, m, nc.scalar.copy)
 
         def store(k, m_lo, m_hi):
-            dst = out[k // H, k % H].rearrange("(m p) d -> p m d", p=P)
+            dst = out[k // H, k % H].rearrange("(p m) d -> p m d", m=M_TILES)
             nc.sync.dma_start(out=dst[:, m_lo:m_hi, :], in_=stage[k][:, m_lo:m_hi, :])
 
         load_a(0, True)
+        load_a(1, False)
         load_g(0, 0)
         load_g(0, 1)
-        load_a(1, False)
         load_a(2, False)
         load_a(3, False)
         load_g(1, 0)
-        a_regroup_scalar(0)
-        a_regroup_vector(0)
-        a_quantise(0)
-        load_a(4, False)
-        for b in range(B):
-            first = b * H
-            for c in range(PASSES):
-                g_regroup(b, c, 2, False)
-                if b == 1 and c == 0:
-                    evict_head(first - 1)
-                g_regroup(b, c, 3, False)
-                g_regroup(b, c, 0, True)
-                g_regroup(b, c, 1, True)
-                g_quantise(b, c, 0)
-                g_quantise(b, c, 1)
-                if b == 0 and c == 0:
-                    load_g(1, 1)
-            if b == 0:
-                a_regroup_scalar(1)
-            else:
-                for k in range(H):
-                    store(k, 0, M_TILES)
-                a_regroup_scalar(first)
-                a_regroup_vector(first)
-                a_quantise(first)
-                a_regroup_scalar(first + 1)
-            multiply(first)
-            for k in range(first + 1, first + H):
-                h = k % H
-                a_regroup_vector(k)
-                if h >= 2:
-                    g_quantise(b, 0, h)
-                    g_quantise(b, 1, h)
-                a_quantise(k)
-                if b == 0:
-                    load_a(k + H, False)
-                evict_head(k - 1)
-                if b == 1:
-                    store(k - 1, 0, M_TILES)
-                if k < first + H - 1:
-                    a_regroup_scalar(k + 1)
-                if k < HEADS - 1:
-                    multiply(k)
-                else:
-                    for c in range(PASSES):
-                        for m in range(M_TILES):
-                            mx_pass(k, m, c)
+        for k in range(2):
+            a_regroup_scalar(k)
+            a_regroup_vector(k)
+            a_quantise(k)
+        for c in range(PASSES):
+            g_regroup(0, c, 2, False)
+            g_regroup(0, c, 3, False)
+            g_regroup(0, c, 0, True)
+            g_regroup(0, c, 1, True)
+            g_quantise(0, c, 0)
+            g_quantise(0, c, 1)
+            if c == 0:
+                load_g(1, 1)
+                load_a(4, False)
+                load_a(5, False)
+        multiply(0)
+        multiply(1)
+        for k in range(2, H):
+            a_regroup_scalar(k)
+            evict_head(k - 2)
+            a_regroup_vector(k)
+            g_quantise(0, 0, k)
+            g_quantise(0, 1, k)
+            a_quantise(k)
+            load_a(k + H, False)
+            multiply(k)
+        for c in range(PASSES):
+            g_regroup(1, c, 2, False)
+            evict_head(2 + c)
+            g_regroup(1, c, 3, False)
+            g_regroup(1, c, 0, True)
+            g_regroup(1, c, 1, True)
+            g_quantise(1, c, 0)
+            g_quantise(1, c, 1)
+        for k in range(H):
+            store(k, 0, M_TILES)
+        a_regroup_scalar(H)
+        a_regroup_vector(H)
+        a_quantise(H)
+        a_regroup_scalar(H + 1)
+        multiply(H)
         last = HEADS - 1
+        for k in range(H + 1, last):
+            a_regroup_vector(k)
+            if k % H >= 2:
+                g_quantise(1, 0, k % H)
+                g_quantise(1, 1, k % H)
+            a_quantise(k)
+            evict_head(k - 1)
+            store(k - 1, 0, M_TILES)
+            a_regroup_scalar(k + 1)
+            multiply(k)
+        for c in range(PASSES):
+            a_regroup_vector_pass(last, c)
+            g_quantise(1, c, last % H)
+            a_quantise_pass(last, c)
+        evict_head(last - 1)
+        store(last - 1, 0, M_TILES)
+        for c in range(PASSES):
+            for m in range(M_TILES):
+                mx_pass(last, m, c)
         for m in range(M_TILES):
             evict(last, m, nc.vector.tensor_copy if m % 2 == 0 else nc.scalar.copy)
             if m % 2 == 1:

@@ -74,24 +74,10 @@ def tile_attentionweightedvalues_kernel(tc, attn_weights, v, batch_size, tgt_len
                 dst = grp_v_pool.tile([P, PACK * S], BF16, name="grp_v", align_bytes=64)
                 grouped[("a", k, c)] = dst
                 if v_rows(k) < P:
-                    nc.scalar.copy(
-                        out=dst[:]
-                        .rearrange("p (m i j) -> p m i j", m=M_TILES, i=P, j=PACK)[:, :, v_rows(k) : P, :]
-                        .rearrange("p m i j -> p i j m"),
-                        in_=a_raw[k][:, c]
-                        .rearrange("p j (i m) -> p j i m", m=M_TILES)[:, :, v_rows(k) : P, :]
-                        .rearrange("p j i m -> p i j m"),
-                    )
+                    regroup(nc.scalar.copy, dst, a_raw[k][:, c], PACK * v_rows(k), S)
 
         def a_regroup_vector_pass(k, c):
-            nc.vector.tensor_copy(
-                out=grouped[("a", k, c)][:]
-                .rearrange("p (mh ml i j) -> p mh ml i j", mh=2, ml=2, i=P, j=PACK)[:, :, :, 0 : v_rows(k), :]
-                .rearrange("p mh ml i j -> p mh i j ml"),
-                in_=a_raw[k][:, c]
-                .rearrange("p j (i mh ml) -> p j i mh ml", mh=2, ml=2)[:, :, 0 : v_rows(k), :, :]
-                .rearrange("p j i mh ml -> p mh i j ml"),
-            )
+            regroup(nc.vector.tensor_copy, grouped[("a", k, c)], a_raw[k][:, c], 0, PACK * v_rows(k))
 
         def a_regroup_vector(k):
             for c in range(PASSES):
@@ -157,7 +143,7 @@ def tile_attentionweightedvalues_kernel(tc, attn_weights, v, batch_size, tgt_len
                 evict(k, m, nc.scalar.copy)
 
         def store(k, m_lo, m_hi):
-            dst = out[k // H, k % H].rearrange("(p m) d -> p m d", m=M_TILES)
+            dst = out[k // H, k % H].rearrange("(m p) d -> p m d", p=P)
             nc.sync.dma_start(out=dst[:, m_lo:m_hi, :], in_=stage[k][:, m_lo:m_hi, :])
 
         load_a(0, True)

@@ -34,7 +34,6 @@ def tile_attentionweightedvalues_kernel(tc, attn_weights, v, batch_size, tgt_len
         g_mx_pool = ctx.enter_context(tc.tile_pool(name="g_mx", bufs=1))
         stage_pool = ctx.enter_context(tc.tile_pool(name="stage", bufs=6))
         psum_pool = ctx.enter_context(tc.psum_pool(name="acc", bufs=8))
-        ctx.enter_context(tc.manual_schedule())
 
         a_raw = {}
         g_raw = {}
@@ -74,10 +73,24 @@ def tile_attentionweightedvalues_kernel(tc, attn_weights, v, batch_size, tgt_len
                 dst = grp_v_pool.tile([P, PACK * S], BF16, name="grp_v", align_bytes=64)
                 grouped[("a", k, c)] = dst
                 if v_rows(k) < P:
-                    regroup(nc.scalar.copy, dst, a_raw[k][:, c], PACK * v_rows(k), S)
+                    nc.scalar.copy(
+                        out=dst[:]
+                        .rearrange("p (m i j) -> p m i j", m=M_TILES, i=P, j=PACK)[:, :, v_rows(k) : P, :]
+                        .rearrange("p m i j -> p i j m"),
+                        in_=a_raw[k][:, c]
+                        .rearrange("p j (i m) -> p j i m", m=M_TILES)[:, :, v_rows(k) : P, :]
+                        .rearrange("p j i m -> p i j m"),
+                    )
 
         def a_regroup_vector_pass(k, c):
-            regroup(nc.vector.tensor_copy, grouped[("a", k, c)], a_raw[k][:, c], 0, PACK * v_rows(k))
+            nc.vector.tensor_copy(
+                out=grouped[("a", k, c)][:]
+                .rearrange("p (mh ml i j) -> p mh ml i j", mh=2, ml=2, i=P, j=PACK)[:, :, :, 0 : v_rows(k), :]
+                .rearrange("p mh ml i j -> p mh i j ml"),
+                in_=a_raw[k][:, c]
+                .rearrange("p j (i mh ml) -> p j i mh ml", mh=2, ml=2)[:, :, 0 : v_rows(k), :, :]
+                .rearrange("p j i mh ml -> p mh i j ml"),
+            )
 
         def a_regroup_vector(k):
             for c in range(PASSES):
@@ -143,7 +156,7 @@ def tile_attentionweightedvalues_kernel(tc, attn_weights, v, batch_size, tgt_len
                 evict(k, m, nc.scalar.copy)
 
         def store(k, m_lo, m_hi):
-            dst = out[k // H, k % H].rearrange("(m p) d -> p m d", p=P)
+            dst = out[k // H, k % H].rearrange("(p m) d -> p m d", m=M_TILES)
             nc.sync.dma_start(out=dst[:, m_lo:m_hi, :], in_=stage[k][:, m_lo:m_hi, :])
 
         load_a(0, True)

from contextlib import ExitStack

import concourse.mybir as mybir

BF16 = mybir.dt.bfloat16
F32 = mybir.dt.float32
U32 = mybir.dt.uint32
U8 = mybir.dt.uint8
E4M3X4 = mybir.dt.float8_e4m3fn_x4
E5M2X4 = mybir.dt.float8_e5m2_x4

P = 128
PACK = 4
B, H, T, S, D = 2, 4, 1024, 512, 512
PASSES = T // (P * PACK)
M_TILES = S // P
HEADS = B * H

FLOPS = 2 * B * H * S * D * T
BYTES = 2 * B * H * T * S + 2 * B * T * H * D + 4 * B * H * S * D

S_ROWS = 28
S_ROWS_BY_HEAD = {0: 44, 1: 44, 4: 0}


def tile_attentionweightedvalues_kernel(tc, attn_weights, v, batch_size, tgt_len, grad_out, out):
    nc = tc.nc
    with ExitStack() as ctx:
        a_raw_pool = ctx.enter_context(tc.tile_pool(name="a_raw", bufs=4))
        g_raw_pool = ctx.enter_context(tc.tile_pool(name="g_raw", bufs=3))
        grp_v_pool = ctx.enter_context(tc.tile_pool(name="grp_v", bufs=6))
        grp_s_pool = ctx.enter_context(tc.tile_pool(name="grp_s", bufs=4))
        a_mx_pool = ctx.enter_context(tc.tile_pool(name="a_mx", bufs=3))
        g_mx_pool = ctx.enter_context(tc.tile_pool(name="g_mx", bufs=1))
        stage_pool = ctx.enter_context(tc.tile_pool(name="stage", bufs=6))
        psum_pool = ctx.enter_context(tc.psum_pool(name="acc", bufs=8))

        a_raw = {}
        g_raw = {}
        grouped = {}
        a_mx = {}
        g_mx = {}
        acc = {}
        stage = {}

        def load_a(k, split):
            raw = a_raw_pool.tile([P, PASSES, PACK, S], BF16, name="a_raw")
            a_raw[k] = raw
            src = attn_weights[k // H, k % H].rearrange("(c p j) w -> p c j w", c=PASSES, p=P, j=PACK)
            if split:
                for c in range(PASSES):
                    nc.sync.dma_start(out=raw[:, c], in_=src[:, c])
            else:
                nc.sync.dma_start(out=raw[:], in_=src)

        def load_g(b, c):
            raw = g_raw_pool.tile([P, PACK, H, D], BF16, name="g_raw")
            g_raw[(b, c)] = raw
            rows = grad_out[b, c * P * PACK : (c + 1) * P * PACK, :]
            nc.sync.dma_start(out=raw[:], in_=rows.rearrange("(p j) (h d) -> p j h d", j=PACK, h=H))

        def regroup(copy, dst, src, lo, hi):
            copy(
                out=dst[:, PACK * lo : PACK * hi].rearrange("p (c i t) -> p c t i", i=4, t=PACK),
                in_=src[:, :, lo:hi].rearrange("p t (c i) -> p c t i", i=4),
            )

        def v_rows(k):
            return P - S_ROWS_BY_HEAD.get(k, S_ROWS)

        def a_regroup_scalar(k):
            for c in range(PASSES):
                dst = grp_v_pool.tile([P, PACK * S], BF16, name="grp_v", align_bytes=64)
                grouped[("a", k, c)] = dst
                if v_rows(k) < P:
                    nc.scalar.copy(
                        out=dst[:]
                        .rearrange("p (m i j) -> p m i j", m=M_TILES, i=P, j=PACK)[:, :, v_rows(k) : P, :]
                        .rearrange("p m i j -> p i j m"),
                        in_=a_raw[k][:, c]
                        .rearrange("p j (i m) -> p j i m", m=M_TILES)[:, :, v_rows(k) : P, :]
                        .rearrange("p j i m -> p i j m"),
                    )

        def a_regroup_vector_pass(k, c):
            nc.vector.tensor_copy(
                out=grouped[("a", k, c)][:]
                .rearrange("p (mh ml i j) -> p mh ml i j", mh=2, ml=2, i=P, j=PACK)[:, :, :, 0 : v_rows(k), :]
                .rearrange("p mh ml i j -> p mh i j ml"),
                in_=a_raw[k][:, c]
                .rearrange("p j (i mh ml) -> p j i mh ml", mh=2, ml=2)[:, :, 0 : v_rows(k), :, :]
                .rearrange("p j i mh ml -> p mh i j ml"),
            )

        def a_regroup_vector(k):
            for c in range(PASSES):
                a_regroup_vector_pass(k, c)

        def a_quantise_pass(k, c):
            if c == 0:
                codes = a_mx_pool.tile([P, PASSES, S], U32, name="a_codes", align_bytes=64)
                scales = a_mx_pool.tile([P, PASSES, S], U8, name="a_scales", align_bytes=64)
                a_mx[k] = (codes, scales)
            codes, scales = a_mx[k]
            nc.vector.quantize_mx(
                out=codes[:, c, :].bitcast(E4M3X4), scales=scales[:, c, :], in_=grouped[("a", k, c)][:]
            )

        def a_quantise(k):
            for c in range(PASSES):
                a_quantise_pass(k, c)

        def g_regroup(b, c, h, on_vector):
            if on_vector:
                dst = grp_v_pool.tile([P, PACK * D], BF16, name="grp_v", align_bytes=64)
                regroup(nc.vector.tensor_copy, dst, g_raw[(b, c)][:, :, h, :], 0, D)
            else:
                dst = grp_s_pool.tile([P, PACK * D], BF16, name="grp_s", align_bytes=64)
                regroup(nc.scalar.copy, dst, g_raw[(b, c)][:, :, h, :], 0, D)
            grouped[("g", b, c, h)] = dst

        def g_quantise(b, c, h):
            codes = g_mx_pool.tile([P, D], U32, name="g_codes_%d_%d_%d" % (b, c, h), align_bytes=64)
            scales = g_mx_pool.tile([P, D], U8, name="g_scales_%d_%d_%d" % (b, c, h), align_bytes=64)
            g_mx[(b, c, h)] = (codes, scales)
            nc.vector.quantize_mx(out=codes[:].bitcast(E5M2X4), scales=scales[:], in_=grouped[("g", b, c, h)][:])

        def mx_pass(k, m, c):
            if c == 0:
                acc[(k, m)] = psum_pool.tile([P, D], F32, name="acc")
            a_codes, a_scales = a_mx[k]
            g_codes, g_scales = g_mx[(k // H, c, k % H)]
            cols = slice(m * P, (m + 1) * P)
            nc.tensor.matmul_mx(
                out=acc[(k, m)][:],
                lhsT=a_codes[:, c, cols].bitcast(E4M3X4),
                lhsT_scale=a_scales[:, c, cols],
                rhs=g_codes[:].bitcast(E5M2X4),
                rhs_scale=g_scales[:],
                start=(c == 0),
                stop=(c == PASSES - 1),
            )

        def multiply(k):
            for m in range(M_TILES):
                for c in range(PASSES):
                    mx_pass(k, m, c)

        def evict(k, m, copy):
            if m == 0:
                stage[k] = stage_pool.tile([P, M_TILES, D], F32, name="stage")
            copy(out=stage[k][:, m, :], in_=acc[(k, m)][:])

        def evict_head(k):
            for m in range(M_TILES):
                evict(k, m, nc.scalar.copy)

        def store(k, m_lo, m_hi):
            dst = out[k // H, k % H].rearrange("(p m) d -> p m d", m=M_TILES)
            nc.sync.dma_start(out=dst[:, m_lo:m_hi, :], in_=stage[k][:, m_lo:m_hi, :])

        load_a(0, True)
        load_a(1, False)
        load_g(0, 0)
        load_g(0, 1)
        load_a(2, False)
        load_a(3, False)
        load_g(1, 0)
        for k in range(2):
            a_regroup_scalar(k)
            a_regroup_vector(k)
            a_quantise(k)
        for c in range(PASSES):
            g_regroup(0, c, 2, False)
            g_regroup(0, c, 3, False)
            g_regroup(0, c, 0, True)
            g_regroup(0, c, 1, True)
            g_quantise(0, c, 0)
            g_quantise(0, c, 1)
            if c == 0:
                load_g(1, 1)
                load_a(4, False)
                load_a(5, False)
        multiply(0)
        multiply(1)
        for k in range(2, H):
            a_regroup_scalar(k)
            evict_head(k - 2)
            a_regroup_vector(k)
            g_quantise(0, 0, k)
            g_quantise(0, 1, k)
            a_quantise(k)
            load_a(k + H, False)
            multiply(k)
        for c in range(PASSES):
            g_regroup(1, c, 2, False)
            evict_head(2 + c)
            g_regroup(1, c, 3, False)
            g_regroup(1, c, 0, True)
            g_regroup(1, c, 1, True)
            g_quantise(1, c, 0)
            g_quantise(1, c, 1)
        for k in range(H):
            store(k, 0, M_TILES)
        a_regroup_scalar(H)
        a_regroup_vector(H)
        a_quantise(H)
        a_regroup_scalar(H + 1)
        multiply(H)
        last = HEADS - 1
        for k in range(H + 1, last):
            a_regroup_vector(k)
            if k % H >= 2:
                g_quantise(1, 0, k % H)
                g_quantise(1, 1, k % H)
            a_quantise(k)
            evict_head(k - 1)
            store(k - 1, 0, M_TILES)
            a_regroup_scalar(k + 1)
            multiply(k)
        for c in range(PASSES):
            a_regroup_vector_pass(last, c)
            g_quantise(1, c, last % H)
            a_quantise_pass(last, c)
        evict_head(last - 1)
        store(last - 1, 0, M_TILES)
        for c in range(PASSES):
            for m in range(M_TILES):
                mx_pass(last, m, c)
        for m in range(M_TILES):
            evict(last, m, nc.vector.tensor_copy if m % 2 == 0 else nc.scalar.copy)
            if m % 2 == 1:
                store(last, m - 1, m + 1)
